import numpy as np
import ml_dtypes


def mxq(x, axis, fmt="e4m3"):
    dtype, down = {"e4m3": (ml_dtypes.float8_e4m3fn, 7), "e5m2": (ml_dtypes.float8_e5m2, 14)}[fmt]
    v = np.moveaxis(np.asarray(x, np.float32).astype(ml_dtypes.bfloat16).astype(np.float64), axis, -1)
    blocks = v.reshape(v.shape[:-1] + (-1, 32))
    amax = np.abs(blocks).max(-1, keepdims=True)
    byte = np.maximum(np.where(amax > 0, np.frexp(amax)[1] - 1 + 127, 0) - down, 1)
    scale = np.exp2(byte - 127.0)
    codes = (blocks / scale).astype(np.float32).astype(dtype).astype(np.float64)
    return np.moveaxis((codes * scale).reshape(v.shape), -1, axis)


WIDE = False


def mx_kscale(k):
    if not WIDE:
        return np.ones(k)
    levels = np.array([18, -18])
    if k % 512:
        return np.exp2(np.random.permutation(np.resize(levels, k // 32))).repeat(32)
    a = np.empty((k // 512, 16))
    for p in range(k // 512):
        a[p, :8] = np.random.permutation(np.resize(levels, 8))
        for g in range(8):
            far = levels[np.abs(levels - a[p, g]) >= 10]
            a[p, g + 8] = far[np.random.randint(len(far))]
    return np.exp2(a.ravel()).repeat(32)


BF16 = ml_dtypes.bfloat16


def bf(x):
    return np.asarray(x, np.float32).astype(BF16)


def f64(x):
    return np.asarray(x).astype(np.float64)


N, NFEAT, NHID = 1024, 512, 512
SPAN = 60.0
LAM = SPAN * np.log(2.0)
AGG = np.sqrt(LAM / (2.0 * N))
GSCALE = 4.0


def setup_inputs():
    u = mx_kscale(N)
    v = mx_kscale(NHID)
    s = mx_kscale(N)
    x0 = bf(np.random.standard_normal((N, NFEAT)))
    adj0 = bf(np.exp2(-SPAN * np.random.uniform(size=(N, N))) * (LAM / N))
    W1_0 = bf(np.random.standard_normal((NFEAT, NHID)) * (0.7 / (AGG * np.sqrt(NFEAT))))
    b1 = bf(np.random.standard_normal(NHID) * 0.3)
    g = bf(np.random.standard_normal((N, NHID)) * np.exp2(np.random.randint(-6, 1, (N, 1))) * GSCALE * u[:, None] * v)
    z = f64(adj0) @ (f64(x0) @ f64(W1_0)) + f64(b1)
    return {
        "x": bf(f64(x0) * s[:, None]),
        "adj": bf(f64(adj0) / u[:, None] / s),
        "W1": bf(f64(W1_0) / v),
        "b1": b1,
        "z": np.asarray(z, np.float32),
        "grad_out": g,
    }


def reference(x, adj, W1, b1, z, grad_out):
    dz2 = f64(grad_out) * (f64(z) > 0.0)
    dh = mxq(f64(adj), 0, "e4m3").T @ mxq(dz2, 0, "e5m2")
    dz1 = dh
    dx = mxq(dz1, 1, "e5m2") @ mxq(f64(W1), 1, "e4m3").T
    dW1 = mxq(f64(x), 0, "e4m3").T @ mxq(dz1, 0, "e5m2")
    return dx, dW1

@@ -1,0 +1,364 @@
+from contextlib import ExitStack
+
+import concourse.mybir as mybir
+from concourse.masks import make_identity
+
+N, F, H = 1024, 512, 512
+P = 128
+FLOPS = 2 * N * N * H + 2 * N * H * F + 2 * F * N * H
+BYTES = 2 * (N * F + N * N + F * H + N * H) + 4 * N * H + 4 * (N * F + F * H)
+
+F32 = mybir.dt.float32
+BF16 = mybir.dt.bfloat16
+U32 = mybir.dt.uint32
+U8 = mybir.dt.uint8
+E4 = mybir.dt.float8_e4m3fn_x4
+E5 = mybir.dt.float8_e5m2_x4
+ALU = mybir.AluOpType
+
+
+def tile_gcn_pa_v_kernel(tc, x, adj, W1, b1, z, grad_out, out_0, out_1):
+    nc = tc.nc
+    with ExitStack() as ctx:
+        sb = ctx.enter_context(tc.tile_pool(name="sb", bufs=1))
+        ps = ctx.enter_context(tc.psum_pool(name="ps", bufs=8))
+        st = ctx.enter_context(tc.tile_pool(name="st", bufs=3))
+
+        def keep(shape, dtype, name):
+            return sb.tile(shape, dtype, name=name, align_bytes=64)
+
+        def bank(dtype=F32, width=512):
+            t = ps.tile([P, width], dtype, name="bank")
+            return t
+
+        ident = keep([P, P], F32, "ident")
+        make_identity(nc, ident[:])
+        identb = keep([P, P], BF16, "identb")
+        make_identity(nc, identb[:])
+
+        adj_raw = [[keep([P, 4, 512], BF16, "adj_raw%d%d" % (g, k)) for k in range(2)] for g in range(2)]
+        adj_il = [[keep([P, 512, 4], BF16, "adj_il%d%d" % (g, h)) for h in range(2)] for g in range(2)]
+        adj_q = [[keep([P, 512], U32, "adj_q%d%d" % (g, h)) for h in range(2)] for g in range(2)]
+        adj_s = [[keep([P, 512], U8, "adj_s%d%d" % (g, h)) for h in range(2)] for g in range(2)]
+        z_sb = [keep([P, 4, H], F32, "z_sb%d" % g) for g in range(2)]
+        g_sb = [keep([P, 4, H], BF16, "g_sb%d" % g) for g in range(2)]
+        dz_il = [keep([P, H, 4], BF16, "dz_il%d" % g) for g in range(2)]
+        dz_q = [keep([P, H], U32, "dz_q%d" % g) for g in range(2)]
+        dz_s = [keep([P, H], U8, "dz_s%d" % g) for g in range(2)]
+        w_raw = keep([P, 4, H], BF16, "w_raw")
+        w_il = keep([P, F, 2], F32, "w_il")
+        w_q = keep([P, F], U32, "w_q")
+        w_s = keep([P, F], U8, "w_s")
+        x_raw = [keep([P, 4, F], BF16, "x_raw%d" % g) for g in range(2)]
+        x_il = [keep([P, F, 4], BF16, "x_il%d" % g) for g in range(2)]
+        x_q = [keep([P, F], U32, "x_q%d" % g) for g in range(2)]
+        x_s = [keep([P, F], U8, "x_s%d" % g) for g in range(2)]
+        dh = [keep([P, 4, H], BF16, "dh%d" % g) for g in range(2)]
+        a_il = [keep([P, 4 * P, 2], F32, "a_il%d" % g) for g in range(2)]
+        a_q = [keep([P, 4 * P], U32, "a_q%d" % g) for g in range(2)]
+        a_s = [keep([P, 4 * P], U8, "a_s%d" % g) for g in range(2)]
+        b_il = [keep([P, H, 4], BF16, "b_il%d" % g) for g in range(2)]
+        b_q = [keep([P, H], U32, "b_q%d" % g) for g in range(2)]
+        b_s = [keep([P, H], U8, "b_s%d" % g) for g in range(2)]
+        o0_sb = [keep([P, 4, F], F32, "o0_sb%d" % g) for g in range(2)]
+        o1_sb = [keep([P, H], F32, "o1_sb%d" % g) for g in range(4)]
+        banks = {}
+
+        def copy(eng, out, in_):
+            if eng == "V":
+                nc.vector.tensor_copy(out=out, in_=in_)
+            else:
+                nc.scalar.copy(out=out, in_=in_)
+
+        adj_v = adj.rearrange("(g p t) j -> g p t j", g=2, t=4)
+        z_v = z.rearrange("(g p t) h -> g p t h", g=2, t=4)
+        g_v = grad_out.rearrange("(g p t) h -> g p t h", g=2, t=4)
+        x_v = x.rearrange("(g p t) f -> g p t f", g=2, t=4)
+        w_v = W1.rearrange("(p t) h -> p t h", t=4)
+        o0_v = out_0.rearrange("(g p t) f -> g p t f", g=2, t=4)
+
+        def ld_adjh(g, G):
+            c = slice(512 * G, 512 * G + 512)
+            nc.sync.dma_start(out=adj_raw[g][G][:], in_=adj_v[g][:, :, c])
+
+        def ld_z(g):
+            nc.sync.dma_start(out=z_sb[g][:], in_=z_v[g])
+
+        def ld_zh(g, k):
+            c = slice(256 * k, 256 * k + 256)
+            nc.sync.dma_start(out=z_sb[g][:, :, c], in_=z_v[g][:, :, c])
+
+        def ld_g(g):
+            nc.sync.dma_start(out=g_sb[g][:], in_=g_v[g])
+
+        def ld_x(g):
+            nc.sync.dma_start(out=x_raw[g][:], in_=x_v[g])
+
+        def ld_W():
+            nc.sync.dma_start(out=w_raw[:], in_=w_v)
+
+        def aI(eng, g, G):
+            src = adj_raw[g][G][:].rearrange("p i (c m j) -> p c j m i", m=2, j=4)
+            dst = adj_il[g][G][:].rearrange("p (j c m) i -> p c j m i", j=4, m=2)
+            copy(eng, dst, src)
+
+        def pI(eng, g, G, u):
+            b = bank(BF16, 1024)
+            banks["I", g, G, u] = b
+            for k in range(2):
+                nc.tensor.matmul(
+                    out=b[:, 512 * k : 512 * k + 512], lhsT=identb[:],
+                    rhs=adj_raw[g][G][:, 2 * k : 2 * k + 2, 256 * u : 256 * u + 256], start=True, stop=True,
+                )
+
+        def cI(eng, g, G, u):
+            src = banks["I", g, G, u][:].rearrange("p (i c m j) -> p c j m i", i=4, m=2, j=4)
+            dst = adj_il[g][G][:].rearrange("p (j c m) i -> p c j m i", j=4, m=2)[:, 32 * u : 32 * u + 32]
+            copy(eng, dst, src)
+
+        def quant(q, s, il, fmt, c=None):
+            if c is None:
+                nc.vector.quantize_mx(out=q[:].bitcast(fmt), scales=s[:], in_=il)
+            else:
+                nc.vector.quantize_mx(out=q[:, c].bitcast(fmt), scales=s[:, c], in_=il)
+
+        def flat(t):
+            return t[:].rearrange("p w j -> p (w j)")
+
+        def aQ(eng, g, G):
+            quant(adj_q[g][G], adj_s[g][G], flat(adj_il[g][G]), E4)
+
+        def dz(eng, g, k):
+            c = slice(256 * k, 256 * k + 256)
+            nc.vector.scalar_tensor_tensor(
+                out=dz_il[g][:, c, :],
+                in0=z_sb[g][:, :, c].rearrange("p t h -> p h t"),
+                scalar=0.0,
+                in1=g_sb[g][:, :, c].rearrange("p t h -> p h t"),
+                op0=ALU.is_gt,
+                op1=ALU.mult,
+            )
+
+        def dQ(eng, g):
+            quant(dz_q[g], dz_s[g], flat(dz_il[g]), E5)
+
+        def WT(eng, i):
+            b = bank()
+            banks["W", i] = b
+            for k in range(2):
+                words = w_raw[:, 2 * i + k, :].bitcast(F32)
+                for u in range(2):
+                    o = 256 * k + 128 * u
+                    nc.tensor.transpose(b[:, o : o + 128], words[:, u::2], ident[:])
+
+        def WC(eng, i):
+            copy(
+                eng,
+                w_il[:].rearrange("p (c t) u -> p c t u", t=4)[:, :, 2 * i : 2 * i + 2, :],
+                banks["W", i][:].rearrange("p (t u c) -> p c t u", t=2, u=2),
+            )
+
+        def WQ(eng):
+            quant(w_q, w_s, flat(w_il).bitcast(BF16), E4)
+
+        def xI(eng, G, k):
+            c = slice(256 * k, 256 * k + 256)
+            copy(eng, x_il[G][:, c, :], x_raw[G][:, :, c].rearrange("p t f -> p f t"))
+
+        def xQ(eng, G):
+            quant(x_q[G], x_s[G], flat(x_il[G]), E4)
+
+        def mm(eng, g, G, t):
+            if g == 0:
+                b0 = bank()
+                banks["h", G, t] = b0
+            b = banks["h", G, t]
+            c = slice(P * t, P * t + P)
+            nc.tensor.matmul_mx(
+                out=b[:], lhsT=adj_q[g][G][:, c].bitcast(E4), lhsT_scale=adj_s[g][G][:, c],
+                rhs=dz_q[g][:].bitcast(E5), rhs_scale=dz_s[g][:], start=(g == 0), stop=(g == 1),
+            )
+
+        def h(eng, G, t):
+            copy(eng, dh[G][:, t, :], banks["h", G, t][:])
+
+        def T(eng, G, q):
+            b = bank()
+            banks["T", G, q] = b
+            for k in range(2):
+                words = dh[G][:, 2 * q + k, :].bitcast(F32)
+                for u in range(2):
+                    o = 256 * k + 128 * u
+                    nc.tensor.transpose(b[:, o : o + 128], words[:, u::2], ident[:])
+
+        def jA(eng, G, q):
+            copy(
+                eng,
+                a_il[G][:].rearrange("p (t m) u -> p t m u", t=4)[:, 2 * q : 2 * q + 2],
+                banks["T", G, q][:].rearrange("p (t u m) -> p t m u", t=2, u=2),
+            )
+
+        def qA(eng, G, q):
+            quant(a_q[G], a_s[G], flat(a_il[G]).bitcast(BF16)[:, 1024 * q : 1024 * q + 1024], E5, slice(256 * q, 256 * q + 256))
+
+        def o0(eng, G, t):
+            b = bank()
+            banks["o0", G, t] = b
+            c = slice(P * t, P * t + P)
+            nc.tensor.matmul_mx(
+                out=b[:], lhsT=a_q[G][:, c].bitcast(E5), lhsT_scale=a_s[G][:, c],
+                rhs=w_q[:].bitcast(E4), rhs_scale=w_s[:], start=True, stop=True,
+            )
+
+        def k0(eng, G, t):
+            copy(eng, o0_sb[G][:, t, :], banks["o0", G, t][:])
+
+        def st0(G, q):
+            c = slice(2 * q, 2 * q + 2)
+            nc.sync.dma_start(out=o0_v[G][:, c, :], in_=o0_sb[G][:, c, :])
+
+        def iB(eng, G, k):
+            c = slice(256 * k, 256 * k + 256)
+            copy(eng, b_il[G][:, c, :], dh[G][:, :, c].rearrange("p t h -> p h t"))
+
+        def qB(eng, G):
+            quant(b_q[G], b_s[G], flat(b_il[G]), E5)
+
+        def o1(eng, G, t):
+            if G == 0:
+                b0 = bank()
+                banks["o1", t] = b0
+            b = banks["o1", t]
+            c = slice(P * t, P * t + P)
+            nc.tensor.matmul_mx(
+                out=b[:], lhsT=x_q[G][:, c].bitcast(E4), lhsT_scale=x_s[G][:, c],
+                rhs=b_q[G][:].bitcast(E5), rhs_scale=b_s[G][:], start=(G == 0), stop=(G == 1),
+            )
+
+        def k1(eng, t):
+            copy(eng, o1_sb[t][:], banks["o1", t][:])
+
+        def st1(t):
+            nc.sync.dma_start(out=out_1[P * t : P * t + P, :], in_=o1_sb[t][:])
+
+        with tc.manual_schedule():
+            ld_adjh(0, 0)
+            ld_g(0)
+            ld_z(0)
+            ld_adjh(1, 0)
+            ld_g(1)
+            ld_z(1)
+            ld_adjh(0, 1)
+            ld_adjh(1, 1)
+            ld_W()
+            ld_x(0)
+            ld_x(1)
+            aI("V", 0, 0)
+            aQ("V", 0, 0)
+            dz("V", 0, 0)
+            dz("V", 0, 1)
+            aI("S", 1, 0)
+            dQ("V", 0)
+            mm("P", 0, 0, 1)
+            mm("P", 0, 0, 2)
+            mm("P", 0, 0, 0)
+            aQ("V", 1, 0)
+            mm("P", 0, 0, 3)
+            dz("V", 1, 0)
+            dz("V", 1, 1)
+            pI("P", 0, 1, 1)
+            pI("P", 0, 1, 0)
+            cI("S", 0, 1, 1)
+            cI("S", 0, 1, 0)
+            pI("P", 1, 1, 1)
+            dQ("V", 1)
+            pI("P", 1, 1, 0)
+            cI("S", 1, 1, 1)
+            aQ("V", 0, 1)
+            mm("P", 1, 0, 2)
+            mm("P", 1, 0, 3)
+            cI("V", 1, 1, 0)
+            h("S", 0, 2)
+            WT("P", 0)
+            aQ("V", 1, 1)
+            xI("S", 0, 0)
+            mm("P", 1, 0, 0)
+            mm("P", 1, 0, 1)
+            xI("V", 0, 1)
+            WT("P", 1)
+            h("V", 0, 3)
+            h("S", 0, 1)
+            mm("P", 0, 1, 0)
+            mm("P", 0, 1, 1)
+            h("S", 0, 0)
+            xQ("V", 0)
+            mm("P", 1, 1, 0)
+            T("P", 0, 1)
+            h("S", 1, 0)
+            WC("V", 0)
+            T("P", 0, 0)
+            xI("V", 1, 1)
+            jA("S", 0, 1)
+            mm("P", 1, 1, 1)
+            WC("S", 1)
+            iB("V", 0, 0)
+            mm("P", 0, 1, 2)
+            mm("P", 0, 1, 3)
+            h("S", 1, 1)
+            mm("P", 1, 1, 2)
+            qA("V", 0, 1)
+            jA("S", 0, 0)
+            WQ("V")
+            mm("P", 1, 1, 3)
+            T("P", 1, 0)
+            h("S", 1, 2)
+            h("V", 1, 3)
+            o0("P", 0, 2)
+            jA("S", 1, 0)
+            o0("P", 0, 3)
+            qA("V", 0, 0)
+            iB("V", 0, 1)
+            k0("S", 0, 2)
+            o0("P", 0, 0)
+            T("P", 1, 1)
+            k0("S", 0, 3)
+            st0(0, 1)
+            qA("V", 1, 0)
+            qB("V", 0)
+            o0("P", 0, 1)
+            jA("S", 1, 1)
+            iB("V", 1, 0)
+            o1("P", 0, 0)
+            k0("S", 0, 0)
+            o0("P", 1, 1)
+            qA("V", 1, 1)
+            k0("S", 0, 1)
+            st0(0, 0)
+            o0("P", 1, 0)
+            xI("V", 1, 0)
+            o0("P", 1, 3)
+            k0("S", 1, 0)
+            o1("P", 0, 1)
+            iB("V", 1, 1)
+            o0("P", 1, 2)
+            k0("S", 1, 1)
+            st0(1, 0)
+            o1("P", 0, 3)
+            xQ("V", 1)
+            o1("P", 0, 2)
+            k0("S", 1, 3)
+            k0("S", 1, 2)
+            st0(1, 1)
+            qB("V", 1)
+            o1("P", 1, 0)
+            o1("P", 1, 3)
+            k1("S", 0)
+            st1(0)
+            o1("P", 1, 1)
+            k1("V", 3)
+            st1(3)
+            o1("P", 1, 2)
+            k1("V", 1)
+            st1(1)
+            k1("S", 2)
+            st1(2)

@@ -3,362 +3,282 @@ from contextlib import ExitStack
 import concourse.mybir as mybir
 from concourse.masks import make_identity
 
-N, F, H = 1024, 512, 512
+NODES, FEATURES, HIDDEN = 1024, 512, 512
 P = 128
-FLOPS = 2 * N * N * H + 2 * N * H * F + 2 * F * N * H
-BYTES = 2 * (N * F + N * N + F * H + N * H) + 4 * N * H + 4 * (N * F + F * H)
+SLOTS = 4
+GROUP = P * SLOTS
+GROUPS = NODES // GROUP
+HALF = GROUP // 2
+QUARTER = GROUP // 4
+
+FLOPS = 2 * NODES * NODES * HIDDEN + 4 * NODES * HIDDEN * FEATURES
+BYTES = (
+    2 * (NODES * FEATURES + NODES * NODES + FEATURES * HIDDEN + NODES * HIDDEN)
+    + 4 * NODES * HIDDEN
+    + 4 * (NODES * FEATURES + FEATURES * HIDDEN)
+)
 
 F32 = mybir.dt.float32
 BF16 = mybir.dt.bfloat16
 U32 = mybir.dt.uint32
 U8 = mybir.dt.uint8
-E4 = mybir.dt.float8_e4m3fn_x4
-E5 = mybir.dt.float8_e5m2_x4
+E4M3 = mybir.dt.float8_e4m3fn_x4
+E5M2 = mybir.dt.float8_e5m2_x4
 ALU = mybir.AluOpType
 
 
 def tile_gcn_pa_v_kernel(tc, x, adj, W1, b1, z, grad_out, out_0, out_1):
     nc = tc.nc
+    on_vector = nc.vector.tensor_copy
+    on_scalar = nc.scalar.copy
+
     with ExitStack() as ctx:
-        sb = ctx.enter_context(tc.tile_pool(name="sb", bufs=1))
-        ps = ctx.enter_context(tc.psum_pool(name="ps", bufs=8))
-        st = ctx.enter_context(tc.tile_pool(name="st", bufs=3))
+        sbuf = ctx.enter_context(tc.tile_pool(name="sbuf", bufs=1))
+        psum = ctx.enter_context(tc.psum_pool(name="psum", bufs=8))
 
-        def keep(shape, dtype, name):
-            return sb.tile(shape, dtype, name=name, align_bytes=64)
+        def keep(name, shape, dtype):
+            return sbuf.tile(shape, dtype, name=name, align_bytes=64)
 
-        def bank(dtype=F32, width=512):
-            t = ps.tile([P, width], dtype, name="bank")
-            return t
+        def codes_and_scales(name):
+            return keep(name + "_codes", [P, GROUP], U32), keep(name + "_scales", [P, GROUP], U8)
 
-        ident = keep([P, P], F32, "ident")
-        make_identity(nc, ident[:])
-        identb = keep([P, P], BF16, "identb")
-        make_identity(nc, identb[:])
+        def pair(name, shape, dtype):
+            return [keep(name + str(g), shape, dtype) for g in range(GROUPS)]
 
-        adj_raw = [[keep([P, 4, 512], BF16, "adj_raw%d%d" % (g, k)) for k in range(2)] for g in range(2)]
-        adj_il = [[keep([P, 512, 4], BF16, "adj_il%d%d" % (g, h)) for h in range(2)] for g in range(2)]
-        adj_q = [[keep([P, 512], U32, "adj_q%d%d" % (g, h)) for h in range(2)] for g in range(2)]
-        adj_s = [[keep([P, 512], U8, "adj_s%d%d" % (g, h)) for h in range(2)] for g in range(2)]
-        z_sb = [keep([P, 4, H], F32, "z_sb%d" % g) for g in range(2)]
-        g_sb = [keep([P, 4, H], BF16, "g_sb%d" % g) for g in range(2)]
-        dz_il = [keep([P, H, 4], BF16, "dz_il%d" % g) for g in range(2)]
-        dz_q = [keep([P, H], U32, "dz_q%d" % g) for g in range(2)]
-        dz_s = [keep([P, H], U8, "dz_s%d" % g) for g in range(2)]
-        w_raw = keep([P, 4, H], BF16, "w_raw")
-        w_il = keep([P, F, 2], F32, "w_il")
-        w_q = keep([P, F], U32, "w_q")
-        w_s = keep([P, F], U8, "w_s")
-        x_raw = [keep([P, 4, F], BF16, "x_raw%d" % g) for g in range(2)]
-        x_il = [keep([P, F, 4], BF16, "x_il%d" % g) for g in range(2)]
-        x_q = [keep([P, F], U32, "x_q%d" % g) for g in range(2)]
-        x_s = [keep([P, F], U8, "x_s%d" % g) for g in range(2)]
-        dh = [keep([P, 4, H], BF16, "dh%d" % g) for g in range(2)]
-        a_il = [keep([P, 4 * P, 2], F32, "a_il%d" % g) for g in range(2)]
-        a_q = [keep([P, 4 * P], U32, "a_q%d" % g) for g in range(2)]
-        a_s = [keep([P, 4 * P], U8, "a_s%d" % g) for g in range(2)]
-        b_il = [keep([P, H, 4], BF16, "b_il%d" % g) for g in range(2)]
-        b_q = [keep([P, H], U32, "b_q%d" % g) for g in range(2)]
-        b_s = [keep([P, H], U8, "b_s%d" % g) for g in range(2)]
-        o0_sb = [keep([P, 4, F], F32, "o0_sb%d" % g) for g in range(2)]
-        o1_sb = [keep([P, H], F32, "o1_sb%d" % g) for g in range(4)]
+        identity = keep("identity", [P, P], F32)
+        make_identity(nc, identity[:])
+
+        adj_raw = pair("adj_raw", [P, SLOTS, NODES], BF16)
+        adj_packed = [pair("adj_packed%d" % r, [P, GROUP, SLOTS], BF16) for r in range(GROUPS)]
+        adj_mx = [[codes_and_scales("adj%d%d" % (r, c)) for c in range(GROUPS)] for r in range(GROUPS)]
+
+        z_raw = pair("z_raw", [P, SLOTS, HIDDEN], F32)
+        grad_raw = pair("grad_raw", [P, SLOTS, HIDDEN], BF16)
+        dz2_packed = pair("dz2_packed", [P, HIDDEN, SLOTS], BF16)
+        dz2_mx = [codes_and_scales("dz2_%d" % r) for r in range(GROUPS)]
+
+        x_raw = pair("x_raw", [P, SLOTS, FEATURES], BF16)
+        x_packed = pair("x_packed", [P, FEATURES, SLOTS], BF16)
+        x_mx = [codes_and_scales("x%d" % c) for c in range(GROUPS)]
+
+        w1_raw = keep("w1_raw", [P, SLOTS, HIDDEN], BF16)
+        w1_packed = keep("w1_packed", [P, FEATURES, SLOTS], BF16)
+        w1_mx = codes_and_scales("w1")
+
+        dz1 = pair("dz1", [P, SLOTS, HIDDEN], BF16)
+        dz1_by_hidden = pair("dz1_by_hidden", [P, GROUP, SLOTS], BF16)
+        dz1_by_hidden_mx = [codes_and_scales("dz1_by_hidden%d" % c) for c in range(GROUPS)]
+        dz1_by_node = pair("dz1_by_node", [P, HIDDEN, SLOTS], BF16)
+        dz1_by_node_mx = [codes_and_scales("dz1_by_node%d" % c) for c in range(GROUPS)]
+
+        out_0_sb = pair("out_0_sb", [P, SLOTS, FEATURES], F32)
+        out_1_sb = [keep("out_1_sb%d" % f, [P, HIDDEN], F32) for f in range(FEATURES // P)]
         banks = {}
 
-        def copy(eng, out, in_):
-            if eng == "V":
-                nc.vector.tensor_copy(out=out, in_=in_)
-            else:
-                nc.scalar.copy(out=out, in_=in_)
+        def open_bank(key):
+            bank = psum.tile([P, 512], F32, name="bank")
+            banks[key] = bank
+            return bank
 
-        adj_v = adj.rearrange("(g p t) j -> g p t j", g=2, t=4)
-        z_v = z.rearrange("(g p t) h -> g p t h", g=2, t=4)
-        g_v = grad_out.rearrange("(g p t) h -> g p t h", g=2, t=4)
-        x_v = x.rearrange("(g p t) f -> g p t f", g=2, t=4)
-        w_v = W1.rearrange("(p t) h -> p t h", t=4)
-        o0_v = out_0.rearrange("(g p t) f -> g p t f", g=2, t=4)
 
-        def ld_adjh(g, G):
-            c = slice(512 * G, 512 * G + 512)
-            nc.sync.dma_start(out=adj_raw[g][G][:], in_=adj_v[g][:, :, c])
+        def by_group(dram):
+            return dram.rearrange("(g p t) w -> g p t w", p=P, t=SLOTS)
 
-        def ld_z(g):
-            nc.sync.dma_start(out=z_sb[g][:], in_=z_v[g])
+        def pack(copy, packed, raw, first, last):
+            cols = slice(QUARTER * first, QUARTER * last)
+            copy(
+                out=packed[:, cols, :].rearrange("p (c i) t -> p c t i", i=4),
+                in_=raw[:, :, cols].rearrange("p t (c i) -> p c t i", i=4),
+            )
 
-        def ld_zh(g, k):
-            c = slice(256 * k, 256 * k + 256)
-            nc.sync.dma_start(out=z_sb[g][:, :, c], in_=z_v[g][:, :, c])
-
-        def ld_g(g):
-            nc.sync.dma_start(out=g_sb[g][:], in_=g_v[g])
-
-        def ld_x(g):
-            nc.sync.dma_start(out=x_raw[g][:], in_=x_v[g])
-
-        def ld_W():
-            nc.sync.dma_start(out=w_raw[:], in_=w_v)
-
-        def aI(eng, g, G):
-            src = adj_raw[g][G][:].rearrange("p i (c m j) -> p c j m i", m=2, j=4)
-            dst = adj_il[g][G][:].rearrange("p (j c m) i -> p c j m i", j=4, m=2)
-            copy(eng, dst, src)
-
-        def pI(eng, g, G, u):
-            b = bank(BF16, 1024)
-            banks["I", g, G, u] = b
+        def transpose_two_tiles(key, raw, q):
+            bank = open_bank(key)
             for k in range(2):
-                nc.tensor.matmul(
-                    out=b[:, 512 * k : 512 * k + 512], lhsT=identb[:],
-                    rhs=adj_raw[g][G][:, 2 * k : 2 * k + 2, 256 * u : 256 * u + 256], start=True, stop=True,
-                )
+                words = raw[:, 2 * q + k, :].bitcast(F32)
+                for u in range(2):
+                    start = P * (2 * k + u)
+                    nc.tensor.transpose(bank[:, start : start + P], words[:, u::2], identity[:])
 
-        def cI(eng, g, G, u):
-            src = banks["I", g, G, u][:].rearrange("p (i c m j) -> p c j m i", i=4, m=2, j=4)
-            dst = adj_il[g][G][:].rearrange("p (j c m) i -> p c j m i", j=4, m=2)[:, 32 * u : 32 * u + 32]
-            copy(eng, dst, src)
+        def quantize(mx, packed, fmt, cols=slice(0, GROUP)):
+            codes, scales = mx
+            nc.vector.quantize_mx(
+                out=codes[:, cols].bitcast(fmt),
+                scales=scales[:, cols],
+                in_=packed[:, cols, :].rearrange("p w t -> p (w t)"),
+            )
 
-        def quant(q, s, il, fmt, c=None):
-            if c is None:
-                nc.vector.quantize_mx(out=q[:].bitcast(fmt), scales=s[:], in_=il)
-            else:
-                nc.vector.quantize_mx(out=q[:, c].bitcast(fmt), scales=s[:, c], in_=il)
+        def multiply(bank, stationary, tile, stationary_fmt, moving, moving_fmt, start, stop):
+            cols = slice(P * tile, P * tile + P)
+            nc.tensor.matmul_mx(
+                out=bank[:],
+                lhsT=stationary[0][:, cols].bitcast(stationary_fmt),
+                lhsT_scale=stationary[1][:, cols],
+                rhs=moving[0][:].bitcast(moving_fmt),
+                rhs_scale=moving[1][:],
+                start=start,
+                stop=stop,
+            )
 
-        def flat(t):
-            return t[:].rearrange("p w j -> p (w j)")
 
-        def aQ(eng, g, G):
-            quant(adj_q[g][G], adj_s[g][G], flat(adj_il[g][G]), E4)
+        def pack_adj(copy, r, c):
+            copy(
+                out=adj_packed[r][c][:].rearrange("p (t a b) i -> p a t b i", t=SLOTS, b=2),
+                in_=adj_raw[r][:, :, GROUP * c : GROUP * c + GROUP].rearrange("p i (a b t) -> p a t b i", b=2, t=SLOTS),
+            )
 
-        def dz(eng, g, k):
-            c = slice(256 * k, 256 * k + 256)
+        def quantize_adj(r, c):
+            quantize(adj_mx[r][c], adj_packed[r][c], E4M3)
+
+
+        def mask_grad(r):
             nc.vector.scalar_tensor_tensor(
-                out=dz_il[g][:, c, :],
-                in0=z_sb[g][:, :, c].rearrange("p t h -> p h t"),
+                out=dz2_packed[r][:],
+                in0=z_raw[r][:].rearrange("p t h -> p h t"),
                 scalar=0.0,
-                in1=g_sb[g][:, :, c].rearrange("p t h -> p h t"),
+                in1=grad_raw[r][:].rearrange("p t h -> p h t"),
                 op0=ALU.is_gt,
                 op1=ALU.mult,
             )
 
-        def dQ(eng, g):
-            quant(dz_q[g], dz_s[g], flat(dz_il[g]), E5)
 
-        def WT(eng, i):
-            b = bank()
-            banks["W", i] = b
-            for k in range(2):
-                words = w_raw[:, 2 * i + k, :].bitcast(F32)
-                for u in range(2):
-                    o = 256 * k + 128 * u
-                    nc.tensor.transpose(b[:, o : o + 128], words[:, u::2], ident[:])
-
-        def WC(eng, i):
+        def collect_w1(copy, q):
+            words = w1_packed[:].rearrange("p f t -> p (f t)").bitcast(F32)
             copy(
-                eng,
-                w_il[:].rearrange("p (c t) u -> p c t u", t=4)[:, :, 2 * i : 2 * i + 2, :],
-                banks["W", i][:].rearrange("p (t u c) -> p c t u", t=2, u=2),
+                out=words.rearrange("p (c t u) -> p c t u", t=SLOTS, u=2)[:, :, 2 * q : 2 * q + 2, :],
+                in_=banks["w1", q][:].rearrange("p (t u c) -> p c t u", t=2, u=2),
             )
 
-        def WQ(eng):
-            quant(w_q, w_s, flat(w_il).bitcast(BF16), E4)
 
-        def xI(eng, G, k):
-            c = slice(256 * k, 256 * k + 256)
-            copy(eng, x_il[G][:, c, :], x_raw[G][:, :, c].rearrange("p t f -> p f t"))
+        def multiply_dh(r, c, t):
+            bank = open_bank(("dh", c, t)) if r == 0 else banks["dh", c, t]
+            multiply(bank, adj_mx[r][c], t, E4M3, dz2_mx[r], E5M2, r == 0, r == GROUPS - 1)
 
-        def xQ(eng, G):
-            quant(x_q[G], x_s[G], flat(x_il[G]), E4)
+        def round_dz1(copy, c, t):
+            copy(out=dz1[c][:, t, :], in_=banks["dh", c, t][:])
 
-        def mm(eng, g, G, t):
-            if g == 0:
-                b0 = bank()
-                banks["h", G, t] = b0
-            b = banks["h", G, t]
-            c = slice(P * t, P * t + P)
-            nc.tensor.matmul_mx(
-                out=b[:], lhsT=adj_q[g][G][:, c].bitcast(E4), lhsT_scale=adj_s[g][G][:, c],
-                rhs=dz_q[g][:].bitcast(E5), rhs_scale=dz_s[g][:], start=(g == 0), stop=(g == 1),
-            )
-
-        def h(eng, G, t):
-            copy(eng, dh[G][:, t, :], banks["h", G, t][:])
-
-        def T(eng, G, q):
-            b = bank()
-            banks["T", G, q] = b
-            for k in range(2):
-                words = dh[G][:, 2 * q + k, :].bitcast(F32)
-                for u in range(2):
-                    o = 256 * k + 128 * u
-                    nc.tensor.transpose(b[:, o : o + 128], words[:, u::2], ident[:])
-
-        def jA(eng, G, q):
+        def collect_by_hidden(copy, c, q):
+            words = dz1_by_hidden[c][:].rearrange("p w t -> p (w t)").bitcast(F32)
             copy(
-                eng,
-                a_il[G][:].rearrange("p (t m) u -> p t m u", t=4)[:, 2 * q : 2 * q + 2],
-                banks["T", G, q][:].rearrange("p (t u m) -> p t m u", t=2, u=2),
+                out=words.rearrange("p (t m u) -> p t m u", t=SLOTS, u=2)[:, 2 * q : 2 * q + 2],
+                in_=banks["dz1", c, q][:].rearrange("p (t u m) -> p t m u", t=2, u=2),
             )
 
-        def qA(eng, G, q):
-            quant(a_q[G], a_s[G], flat(a_il[G]).bitcast(BF16)[:, 1024 * q : 1024 * q + 1024], E5, slice(256 * q, 256 * q + 256))
+        def quantize_by_hidden(c, q):
+            quantize(dz1_by_hidden_mx[c], dz1_by_hidden[c], E5M2, slice(HALF * q, HALF * q + HALF))
 
-        def o0(eng, G, t):
-            b = bank()
-            banks["o0", G, t] = b
-            c = slice(P * t, P * t + P)
-            nc.tensor.matmul_mx(
-                out=b[:], lhsT=a_q[G][:, c].bitcast(E5), lhsT_scale=a_s[G][:, c],
-                rhs=w_q[:].bitcast(E4), rhs_scale=w_s[:], start=True, stop=True,
-            )
 
-        def k0(eng, G, t):
-            copy(eng, o0_sb[G][:, t, :], banks["o0", G, t][:])
+        def multiply_out_0(c, t):
+            multiply(open_bank(("out_0", c, t)), dz1_by_hidden_mx[c], t, E5M2, w1_mx, E4M3, True, True)
 
-        def st0(G, q):
-            c = slice(2 * q, 2 * q + 2)
-            nc.sync.dma_start(out=o0_v[G][:, c, :], in_=o0_sb[G][:, c, :])
+        def collect_out_0(copy, c, t):
+            copy(out=out_0_sb[c][:, t, :], in_=banks["out_0", c, t][:])
+            nc.sync.dma_start(out=by_group(out_0)[c][:, t, :], in_=out_0_sb[c][:, t, :])
 
-        def iB(eng, G, k):
-            c = slice(256 * k, 256 * k + 256)
-            copy(eng, b_il[G][:, c, :], dh[G][:, :, c].rearrange("p t h -> p h t"))
+        def multiply_out_1(c, f):
+            bank = open_bank(("out_1", f)) if c == 0 else banks["out_1", f]
+            multiply(bank, x_mx[c], f, E4M3, dz1_by_node_mx[c], E5M2, c == 0, c == GROUPS - 1)
 
-        def qB(eng, G):
-            quant(b_q[G], b_s[G], flat(b_il[G]), E5)
-
-        def o1(eng, G, t):
-            if G == 0:
-                b0 = bank()
-                banks["o1", t] = b0
-            b = banks["o1", t]
-            c = slice(P * t, P * t + P)
-            nc.tensor.matmul_mx(
-                out=b[:], lhsT=x_q[G][:, c].bitcast(E4), lhsT_scale=x_s[G][:, c],
-                rhs=b_q[G][:].bitcast(E5), rhs_scale=b_s[G][:], start=(G == 0), stop=(G == 1),
-            )
-
-        def k1(eng, t):
-            copy(eng, o1_sb[t][:], banks["o1", t][:])
-
-        def st1(t):
-            nc.sync.dma_start(out=out_1[P * t : P * t + P, :], in_=o1_sb[t][:])
+        def collect_out_1(copy, f):
+            copy(out=out_1_sb[f][:], in_=banks["out_1", f][:])
+            nc.sync.dma_start(out=out_1[P * f : P * f + P, :], in_=out_1_sb[f][:])
 
         with tc.manual_schedule():
-            ld_adjh(0, 0)
-            ld_g(0)
-            ld_z(0)
-            ld_adjh(1, 0)
-            ld_g(1)
-            ld_z(1)
-            ld_adjh(0, 1)
-            ld_adjh(1, 1)
-            ld_W()
-            ld_x(0)
-            ld_x(1)
-            aI("V", 0, 0)
-            aQ("V", 0, 0)
-            dz("V", 0, 0)
-            dz("V", 0, 1)
-            aI("S", 1, 0)
-            dQ("V", 0)
-            mm("P", 0, 0, 1)
-            mm("P", 0, 0, 2)
-            mm("P", 0, 0, 0)
-            aQ("V", 1, 0)
-            mm("P", 0, 0, 3)
-            dz("V", 1, 0)
-            dz("V", 1, 1)
-            pI("P", 0, 1, 1)
-            pI("P", 0, 1, 0)
-            cI("S", 0, 1, 1)
-            cI("S", 0, 1, 0)
-            pI("P", 1, 1, 1)
-            dQ("V", 1)
-            pI("P", 1, 1, 0)
-            cI("S", 1, 1, 1)
-            aQ("V", 0, 1)
-            mm("P", 1, 0, 2)
-            mm("P", 1, 0, 3)
-            cI("V", 1, 1, 0)
-            h("S", 0, 2)
-            WT("P", 0)
-            aQ("V", 1, 1)
-            xI("S", 0, 0)
-            mm("P", 1, 0, 0)
-            mm("P", 1, 0, 1)
-            xI("V", 0, 1)
-            WT("P", 1)
-            h("V", 0, 3)
-            h("S", 0, 1)
-            mm("P", 0, 1, 0)
-            mm("P", 0, 1, 1)
-            h("S", 0, 0)
-            xQ("V", 0)
-            mm("P", 1, 1, 0)
-            T("P", 0, 1)
-            h("S", 1, 0)
-            WC("V", 0)
-            T("P", 0, 0)
-            xI("V", 1, 1)
-            jA("S", 0, 1)
-            mm("P", 1, 1, 1)
-            WC("S", 1)
-            iB("V", 0, 0)
-            mm("P", 0, 1, 2)
-            mm("P", 0, 1, 3)
-            h("S", 1, 1)
-            mm("P", 1, 1, 2)
-            qA("V", 0, 1)
-            jA("S", 0, 0)
-            WQ("V")
-            mm("P", 1, 1, 3)
-            T("P", 1, 0)
-            h("S", 1, 2)
-            h("V", 1, 3)
-            o0("P", 0, 2)
-            jA("S", 1, 0)
-            o0("P", 0, 3)
-            qA("V", 0, 0)
-            iB("V", 0, 1)
-            k0("S", 0, 2)
-            o0("P", 0, 0)
-            T("P", 1, 1)
-            k0("S", 0, 3)
-            st0(0, 1)
-            qA("V", 1, 0)
-            qB("V", 0)
-            o0("P", 0, 1)
-            jA("S", 1, 1)
-            iB("V", 1, 0)
-            o1("P", 0, 0)
-            k0("S", 0, 0)
-            o0("P", 1, 1)
-            qA("V", 1, 1)
-            k0("S", 0, 1)
-            st0(0, 0)
-            o0("P", 1, 0)
-            xI("V", 1, 0)
-            o0("P", 1, 3)
-            k0("S", 1, 0)
-            o1("P", 0, 1)
-            iB("V", 1, 1)
-            o0("P", 1, 2)
-            k0("S", 1, 1)
-            st0(1, 0)
-            o1("P", 0, 3)
-            xQ("V", 1)
-            o1("P", 0, 2)
-            k0("S", 1, 3)
-            k0("S", 1, 2)
-            st0(1, 1)
-            qB("V", 1)
-            o1("P", 1, 0)
-            o1("P", 1, 3)
-            k1("S", 0)
-            st1(0)
-            o1("P", 1, 1)
-            k1("V", 3)
-            st1(3)
-            o1("P", 1, 2)
-            k1("V", 1)
-            st1(1)
-            k1("S", 2)
-            st1(2)
+            for r in range(GROUPS):
+                nc.sync.dma_start(out=grad_raw[r][:], in_=by_group(grad_out)[r])
+                nc.sync.dma_start(out=z_raw[r][:], in_=by_group(z)[r])
+                nc.sync.dma_start(out=adj_raw[r][:], in_=by_group(adj)[r])
+            nc.sync.dma_start(out=w1_raw[:], in_=by_group(W1)[0])
+            for c in range(GROUPS):
+                nc.sync.dma_start(out=x_raw[c][:], in_=by_group(x)[c])
+
+            mask_grad(0)
+            pack_adj(on_scalar, 0, 1)
+            pack_adj(on_vector, 0, 0)
+            quantize(dz2_mx[0], dz2_packed[0], E5M2)
+            for c in range(GROUPS):
+                quantize_adj(0, c)
+            for t in range(SLOTS):
+                multiply_dh(0, 0, t)
+            for t in range(2):
+                multiply_dh(0, 1, t)
+
+            mask_grad(1)
+            pack_adj(on_scalar, 1, 1)
+            pack_adj(on_vector, 1, 0)
+            quantize(dz2_mx[1], dz2_packed[1], E5M2)
+            quantize_adj(1, 0)
+            for q in range(2):
+                transpose_two_tiles(("w1", q), w1_raw, q)
+            for t in range(SLOTS):
+                multiply_dh(1, 0, t)
+
+            pack(on_vector, x_packed[0], x_raw[0], 0, 1)
+            quantize_adj(1, 1)
+            collect_w1(on_scalar, 0)
+            pack(on_scalar, x_packed[0], x_raw[0], 3, 4)
+            collect_w1(on_scalar, 1)
+            pack(on_vector, x_packed[1], x_raw[1], 0, 3)
+            for t in range(2):
+                multiply_dh(1, 1, t)
+            for t in range(2, SLOTS):
+                multiply_dh(0, 1, t)
+            round_dz1(on_vector, 0, 0)
+            for t in range(1, SLOTS):
+                round_dz1(on_scalar, 0, t)
+            transpose_two_tiles(("dz1", 0, 0), dz1[0], 0)
+            for t in range(2, SLOTS):
+                multiply_dh(1, 1, t)
+            pack(on_vector, x_packed[0], x_raw[0], 1, 3)
+
+            round_dz1(on_vector, 1, 0)
+            round_dz1(on_scalar, 1, 1)
+            transpose_two_tiles(("dz1", 1, 0), dz1[1], 0)
+            transpose_two_tiles(("dz1", 0, 1), dz1[0], 1)
+            pack(on_vector, dz1_by_node[0], dz1[0], 0, 2)
+            collect_by_hidden(on_scalar, 0, 0)
+            for t in range(2, SLOTS):
+                round_dz1(on_scalar, 1, t)
+            quantize(w1_mx, w1_packed, E4M3)
+            quantize_by_hidden(0, 0)
+            multiply_out_0(0, 0)
+            pack(on_vector, dz1_by_node[0], dz1[0], 2, 4)
+            pack(on_vector, x_packed[1], x_raw[1], 3, 4)
+
+            collect_by_hidden(on_scalar, 1, 0)
+            collect_by_hidden(on_scalar, 0, 1)
+            pack(on_vector, dz1_by_node[1], dz1[1], 0, 1)
+            quantize_by_hidden(1, 0)
+            quantize_by_hidden(0, 1)
+            transpose_two_tiles(("dz1", 1, 1), dz1[1], 1)
+            multiply_out_0(0, 1)
+            multiply_out_0(1, 0)
+            for t in range(2, SLOTS):
+                multiply_out_0(0, t)
+            multiply_out_0(1, 1)
+            pack(on_vector, dz1_by_node[1], dz1[1], 1, 3)
+            for t in range(2):
+                collect_out_0(on_scalar, 0, t)
+            collect_out_0(on_scalar, 1, 0)
+            collect_by_hidden(on_scalar, 1, 1)
+            quantize(x_mx[0], x_packed[0], E4M3)
+            quantize(dz1_by_node_mx[0], dz1_by_node[0], E5M2)
+            pack(on_vector, dz1_by_node[1], dz1[1], 3, 4)
+            quantize_by_hidden(1, 1)
+            quantize(x_mx[1], x_packed[1], E4M3)
+            quantize(dz1_by_node_mx[1], dz1_by_node[1], E5M2)
+
+            for f in range(2):
+                multiply_out_1(0, f)
+            for t in range(2, SLOTS):
+                multiply_out_0(1, t)
+            for f in range(2, FEATURES // P):
+                multiply_out_1(0, f)
+            for f in range(FEATURES // P):
+                multiply_out_1(1, f)
+            for t in range(2, SLOTS):
+                collect_out_0(on_scalar, 0, t)
+            for t in range(1, 3):
+                collect_out_0(on_scalar, 1, t)
+            collect_out_0(on_vector, 1, 3)
+            for f in range(FEATURES // P):
+                collect_out_1(on_scalar if f < 3 else on_vector, f)

from contextlib import ExitStack

import concourse.mybir as mybir
from concourse.masks import make_identity

NODES, FEATURES, HIDDEN = 1024, 512, 512
P = 128
SLOTS = 4
GROUP = P * SLOTS
GROUPS = NODES // GROUP
HALF = GROUP // 2
QUARTER = GROUP // 4

FLOPS = 2 * NODES * NODES * HIDDEN + 4 * NODES * HIDDEN * FEATURES
BYTES = (
    2 * (NODES * FEATURES + NODES * NODES + FEATURES * HIDDEN + NODES * HIDDEN)
    + 4 * NODES * HIDDEN
    + 4 * (NODES * FEATURES + FEATURES * HIDDEN)
)

F32 = mybir.dt.float32
BF16 = mybir.dt.bfloat16
U32 = mybir.dt.uint32
U8 = mybir.dt.uint8
E4M3 = mybir.dt.float8_e4m3fn_x4
E5M2 = mybir.dt.float8_e5m2_x4
ALU = mybir.AluOpType


def tile_gcn_pa_v_kernel(tc, x, adj, W1, b1, z, grad_out, out_0, out_1):
    nc = tc.nc
    on_vector = nc.vector.tensor_copy
    on_scalar = nc.scalar.copy

    with ExitStack() as ctx:
        sbuf = ctx.enter_context(tc.tile_pool(name="sbuf", bufs=1))
        psum = ctx.enter_context(tc.psum_pool(name="psum", bufs=8))

        def keep(name, shape, dtype):
            return sbuf.tile(shape, dtype, name=name, align_bytes=64)

        def codes_and_scales(name):
            return keep(name + "_codes", [P, GROUP], U32), keep(name + "_scales", [P, GROUP], U8)

        def pair(name, shape, dtype):
            return [keep(name + str(g), shape, dtype) for g in range(GROUPS)]

        identity = keep("identity", [P, P], F32)
        make_identity(nc, identity[:])

        adj_raw = pair("adj_raw", [P, SLOTS, NODES], BF16)
        adj_packed = [pair("adj_packed%d" % r, [P, GROUP, SLOTS], BF16) for r in range(GROUPS)]
        adj_mx = [[codes_and_scales("adj%d%d" % (r, c)) for c in range(GROUPS)] for r in range(GROUPS)]

        z_raw = pair("z_raw", [P, SLOTS, HIDDEN], F32)
        grad_raw = pair("grad_raw", [P, SLOTS, HIDDEN], BF16)
        dz2_packed = pair("dz2_packed", [P, HIDDEN, SLOTS], BF16)
        dz2_mx = [codes_and_scales("dz2_%d" % r) for r in range(GROUPS)]

        x_raw = pair("x_raw", [P, SLOTS, FEATURES], BF16)
        x_packed = pair("x_packed", [P, FEATURES, SLOTS], BF16)
        x_mx = [codes_and_scales("x%d" % c) for c in range(GROUPS)]

        w1_raw = keep("w1_raw", [P, SLOTS, HIDDEN], BF16)
        w1_packed = keep("w1_packed", [P, FEATURES, SLOTS], BF16)
        w1_mx = codes_and_scales("w1")

        dz1 = pair("dz1", [P, SLOTS, HIDDEN], BF16)
        dz1_by_hidden = pair("dz1_by_hidden", [P, GROUP, SLOTS], BF16)
        dz1_by_hidden_mx = [codes_and_scales("dz1_by_hidden%d" % c) for c in range(GROUPS)]
        dz1_by_node = pair("dz1_by_node", [P, HIDDEN, SLOTS], BF16)
        dz1_by_node_mx = [codes_and_scales("dz1_by_node%d" % c) for c in range(GROUPS)]

        out_0_sb = pair("out_0_sb", [P, SLOTS, FEATURES], F32)
        out_1_sb = [keep("out_1_sb%d" % f, [P, HIDDEN], F32) for f in range(FEATURES // P)]
        banks = {}

        def open_bank(key):
            bank = psum.tile([P, 512], F32, name="bank")
            banks[key] = bank
            return bank


        def by_group(dram):
            return dram.rearrange("(g p t) w -> g p t w", p=P, t=SLOTS)

        def pack(copy, packed, raw, first, last):
            cols = slice(QUARTER * first, QUARTER * last)
            copy(
                out=packed[:, cols, :].rearrange("p (c i) t -> p c t i", i=4),
                in_=raw[:, :, cols].rearrange("p t (c i) -> p c t i", i=4),
            )

        def transpose_two_tiles(key, raw, q):
            bank = open_bank(key)
            for k in range(2):
                words = raw[:, 2 * q + k, :].bitcast(F32)
                for u in range(2):
                    start = P * (2 * k + u)
                    nc.tensor.transpose(bank[:, start : start + P], words[:, u::2], identity[:])

        def quantize(mx, packed, fmt, cols=slice(0, GROUP)):
            codes, scales = mx
            nc.vector.quantize_mx(
                out=codes[:, cols].bitcast(fmt),
                scales=scales[:, cols],
                in_=packed[:, cols, :].rearrange("p w t -> p (w t)"),
            )

        def multiply(bank, stationary, tile, stationary_fmt, moving, moving_fmt, start, stop):
            cols = slice(P * tile, P * tile + P)
            nc.tensor.matmul_mx(
                out=bank[:],
                lhsT=stationary[0][:, cols].bitcast(stationary_fmt),
                lhsT_scale=stationary[1][:, cols],
                rhs=moving[0][:].bitcast(moving_fmt),
                rhs_scale=moving[1][:],
                start=start,
                stop=stop,
            )


        def pack_adj(copy, r, c):
            copy(
                out=adj_packed[r][c][:].rearrange("p (t a b) i -> p a t b i", t=SLOTS, b=2),
                in_=adj_raw[r][:, :, GROUP * c : GROUP * c + GROUP].rearrange("p i (a b t) -> p a t b i", b=2, t=SLOTS),
            )

        def quantize_adj(r, c):
            quantize(adj_mx[r][c], adj_packed[r][c], E4M3)


        def mask_grad(r):
            nc.vector.scalar_tensor_tensor(
                out=dz2_packed[r][:],
                in0=z_raw[r][:].rearrange("p t h -> p h t"),
                scalar=0.0,
                in1=grad_raw[r][:].rearrange("p t h -> p h t"),
                op0=ALU.is_gt,
                op1=ALU.mult,
            )


        def collect_w1(copy, q):
            words = w1_packed[:].rearrange("p f t -> p (f t)").bitcast(F32)
            copy(
                out=words.rearrange("p (c t u) -> p c t u", t=SLOTS, u=2)[:, :, 2 * q : 2 * q + 2, :],
                in_=banks["w1", q][:].rearrange("p (t u c) -> p c t u", t=2, u=2),
            )


        def multiply_dh(r, c, t):
            bank = open_bank(("dh", c, t)) if r == 0 else banks["dh", c, t]
            multiply(bank, adj_mx[r][c], t, E4M3, dz2_mx[r], E5M2, r == 0, r == GROUPS - 1)

        def round_dz1(copy, c, t):
            copy(out=dz1[c][:, t, :], in_=banks["dh", c, t][:])

        def collect_by_hidden(copy, c, q):
            words = dz1_by_hidden[c][:].rearrange("p w t -> p (w t)").bitcast(F32)
            copy(
                out=words.rearrange("p (t m u) -> p t m u", t=SLOTS, u=2)[:, 2 * q : 2 * q + 2],
                in_=banks["dz1", c, q][:].rearrange("p (t u m) -> p t m u", t=2, u=2),
            )

        def quantize_by_hidden(c, q):
            quantize(dz1_by_hidden_mx[c], dz1_by_hidden[c], E5M2, slice(HALF * q, HALF * q + HALF))


        def multiply_out_0(c, t):
            multiply(open_bank(("out_0", c, t)), dz1_by_hidden_mx[c], t, E5M2, w1_mx, E4M3, True, True)

        def collect_out_0(copy, c, t):
            copy(out=out_0_sb[c][:, t, :], in_=banks["out_0", c, t][:])
            nc.sync.dma_start(out=by_group(out_0)[c][:, t, :], in_=out_0_sb[c][:, t, :])

        def multiply_out_1(c, f):
            bank = open_bank(("out_1", f)) if c == 0 else banks["out_1", f]
            multiply(bank, x_mx[c], f, E4M3, dz1_by_node_mx[c], E5M2, c == 0, c == GROUPS - 1)

        def collect_out_1(copy, f):
            copy(out=out_1_sb[f][:], in_=banks["out_1", f][:])
            nc.sync.dma_start(out=out_1[P * f : P * f + P, :], in_=out_1_sb[f][:])

        with tc.manual_schedule():
            for r in range(GROUPS):
                nc.sync.dma_start(out=grad_raw[r][:], in_=by_group(grad_out)[r])
                nc.sync.dma_start(out=z_raw[r][:], in_=by_group(z)[r])
                nc.sync.dma_start(out=adj_raw[r][:], in_=by_group(adj)[r])
            nc.sync.dma_start(out=w1_raw[:], in_=by_group(W1)[0])
            for c in range(GROUPS):
                nc.sync.dma_start(out=x_raw[c][:], in_=by_group(x)[c])

            mask_grad(0)
            pack_adj(on_scalar, 0, 1)
            pack_adj(on_vector, 0, 0)
            quantize(dz2_mx[0], dz2_packed[0], E5M2)
            for c in range(GROUPS):
                quantize_adj(0, c)
            for t in range(SLOTS):
                multiply_dh(0, 0, t)
            for t in range(2):
                multiply_dh(0, 1, t)

            mask_grad(1)
            pack_adj(on_scalar, 1, 1)
            pack_adj(on_vector, 1, 0)
            quantize(dz2_mx[1], dz2_packed[1], E5M2)
            quantize_adj(1, 0)
            for q in range(2):
                transpose_two_tiles(("w1", q), w1_raw, q)
            for t in range(SLOTS):
                multiply_dh(1, 0, t)

            pack(on_vector, x_packed[0], x_raw[0], 0, 1)
            quantize_adj(1, 1)
            collect_w1(on_scalar, 0)
            pack(on_scalar, x_packed[0], x_raw[0], 3, 4)
            collect_w1(on_scalar, 1)
            pack(on_vector, x_packed[1], x_raw[1], 0, 3)
            for t in range(2):
                multiply_dh(1, 1, t)
            for t in range(2, SLOTS):
                multiply_dh(0, 1, t)
            round_dz1(on_vector, 0, 0)
            for t in range(1, SLOTS):
                round_dz1(on_scalar, 0, t)
            transpose_two_tiles(("dz1", 0, 0), dz1[0], 0)
            for t in range(2, SLOTS):
                multiply_dh(1, 1, t)
            pack(on_vector, x_packed[0], x_raw[0], 1, 3)

            round_dz1(on_vector, 1, 0)
            round_dz1(on_scalar, 1, 1)
            transpose_two_tiles(("dz1", 1, 0), dz1[1], 0)
            transpose_two_tiles(("dz1", 0, 1), dz1[0], 1)
            pack(on_vector, dz1_by_node[0], dz1[0], 0, 2)
            collect_by_hidden(on_scalar, 0, 0)
            for t in range(2, SLOTS):
                round_dz1(on_scalar, 1, t)
            quantize(w1_mx, w1_packed, E4M3)
            quantize_by_hidden(0, 0)
            multiply_out_0(0, 0)
            pack(on_vector, dz1_by_node[0], dz1[0], 2, 4)
            pack(on_vector, x_packed[1], x_raw[1], 3, 4)

            collect_by_hidden(on_scalar, 1, 0)
            collect_by_hidden(on_scalar, 0, 1)
            pack(on_vector, dz1_by_node[1], dz1[1], 0, 1)
            quantize_by_hidden(1, 0)
            quantize_by_hidden(0, 1)
            transpose_two_tiles(("dz1", 1, 1), dz1[1], 1)
            multiply_out_0(0, 1)
            multiply_out_0(1, 0)
            for t in range(2, SLOTS):
                multiply_out_0(0, t)
            multiply_out_0(1, 1)
            pack(on_vector, dz1_by_node[1], dz1[1], 1, 3)
            for t in range(2):
                collect_out_0(on_scalar, 0, t)
            collect_out_0(on_scalar, 1, 0)
            collect_by_hidden(on_scalar, 1, 1)
            quantize(x_mx[0], x_packed[0], E4M3)
            quantize(dz1_by_node_mx[0], dz1_by_node[0], E5M2)
            pack(on_vector, dz1_by_node[1], dz1[1], 3, 4)
            quantize_by_hidden(1, 1)
            quantize(x_mx[1], x_packed[1], E4M3)
            quantize(dz1_by_node_mx[1], dz1_by_node[1], E5M2)

            for f in range(2):
                multiply_out_1(0, f)
            for t in range(2, SLOTS):
                multiply_out_0(1, t)
            for f in range(2, FEATURES // P):
                multiply_out_1(0, f)
            for f in range(FEATURES // P):
                multiply_out_1(1, f)
            for t in range(2, SLOTS):
                collect_out_0(on_scalar, 0, t)
            for t in range(1, 3):
                collect_out_0(on_scalar, 1, t)
            collect_out_0(on_vector, 1, 3)
            for f in range(FEATURES // P):
                collect_out_1(on_scalar if f < 3 else on_vector, f)
